import numpy as np
import ml_dtypes


def mxq(x, axis, fmt="e4m3"):
    dtype, down = {"e4m3": (ml_dtypes.float8_e4m3fn, 7), "e5m2": (ml_dtypes.float8_e5m2, 14)}[fmt]
    v = np.moveaxis(np.asarray(x, np.float32).astype(ml_dtypes.bfloat16).astype(np.float64), axis, -1)
    blocks = v.reshape(v.shape[:-1] + (-1, 32))
    amax = np.abs(blocks).max(-1, keepdims=True)
    byte = np.maximum(np.where(amax > 0, np.frexp(amax)[1] - 1 + 127, 0) - down, 1)
    scale = np.exp2(byte - 127.0)
    codes = (blocks / scale).astype(np.float32).astype(dtype).astype(np.float64)
    return np.moveaxis((codes * scale).reshape(v.shape), -1, axis)


WIDE = False


def mx_kscale(k):
    if not WIDE:
        return np.ones(k)
    levels = np.array([10, -10, 5, -5, 0])
    if k % 512:
        return np.exp2(np.random.permutation(np.resize(levels, k // 32))).repeat(32)
    a = np.empty((k // 512, 16))
    for p in range(k // 512):
        a[p, :8] = np.random.permutation(np.resize(levels, 8))
        for g in range(8):
            far = levels[np.abs(levels - a[p, g]) >= 10]
            a[p, g + 8] = far[np.random.randint(len(far))]
    return np.exp2(a.ravel()).repeat(32)


BF16 = ml_dtypes.bfloat16


def bf(x):
    return np.asarray(x, np.float32).astype(BF16)


def f64(x):
    return np.asarray(x).astype(np.float64)


B, HW, C, HID, WS, SS, HEADS = 1, 32, 1024, 2048, 8, 4, 16
L = HW * HW
NH = HW // WS
EPS = 1e-5


def adain(x, scale, shift):
    m = x.mean(2, keepdims=True)
    s = np.std(x, axis=2, keepdims=True, ddof=1) + EPS
    return (x - m) / s * scale + shift


def setup_inputs():
    s = mx_kscale(C)
    return {"o_attn": bf(0.4 * np.random.standard_normal((NH * NH * B, WS * WS, C)) * s),
            "out_w": bf(np.random.standard_normal((C, C)) / np.sqrt(C) / s[None, :]),
            "out_b": bf(0.1 * np.random.standard_normal(C)),
            "ada1_scale": bf(1.0 + 0.1 * np.random.standard_normal((1, L, 1))),
            "ada1_shift": bf(0.1 * np.random.standard_normal((1, L, 1))),
            "x": bf(np.random.standard_normal((B, L, C)))}


def core(o_attn, out_w, out_b, ada1_scale, ada1_shift, x):
    a = (mxq(f64(o_attn), 2, "e4m3") @ mxq(f64(out_w), 1, "e4m3").T) + f64(out_b)
    a = np.swapaxes(a.reshape(B, NH, NH, WS, WS, C), 2, 3).reshape(B, HW, HW, C)
    a = np.roll(a, (SS, SS), axis=(1, 2)).reshape(B, L, C)
    return f64(x) + adain(a, f64(ada1_scale), f64(ada1_shift))


def e4m3fn_bytes(y):
    return np.clip(np.asarray(y, np.float64), -448.0, 448.0).astype(np.float32).astype(ml_dtypes.float8_e4m3fn).view(np.uint8)


Y_SCALE = 150.0


def reference(o_attn, out_w, out_b, ada1_scale, ada1_shift, x):
    out = core(o_attn, out_w, out_b, ada1_scale, ada1_shift, x)
    return out, e4m3fn_bytes(out * Y_SCALE)

@@ -1,0 +1,292 @@
+from contextlib import ExitStack
+
+import concourse.mybir as mybir
+from concourse.masks import make_identity
+
+FLOPS = 2 * 1024 * 1024 * 1024
+
+F32 = mybir.dt.float32
+BF16 = mybir.dt.bfloat16
+U32 = mybir.dt.uint32
+U8 = mybir.dt.uint8
+FP8X4 = mybir.dt.float8_e4m3fn_x4
+FP8 = mybir.dt.float8_e4m3fn
+ALU = mybir.AluOpType
+ACT = mybir.ActivationFunctionType
+
+P = 128
+C = 1024
+EPS = 1e-5
+Y_SCALE = 150.0
+
+
+def tile_swintransformerblock_pb_kernel(tc, o_attn, out_w, out_b, ada1_scale, ada1_shift, x, out_0, out_1):
+    nc = tc.nc
+    o_flat = o_attn.flatten_outer_dims()
+    x_flat = x.flatten_outer_dims()
+    y_flat = out_0.flatten_outer_dims()
+    yb_flat = out_1.flatten_outer_dims()
+
+    with ExitStack() as ctx:
+        const = ctx.enter_context(tc.tile_pool(name="const", bufs=1))
+        raw = ctx.enter_context(tc.tile_pool(name="raw", bufs=1))
+        agrp = ctx.enter_context(tc.tile_pool(name="agrp", bufs=2))
+        work = ctx.enter_context(tc.tile_pool(name="work", bufs=3))
+        stat = ctx.enter_context(tc.tile_pool(name="stat", bufs=6))
+        ps_t = ctx.enter_context(tc.psum_pool(name="ps_t", bufs=4))
+        ps_a = ctx.enter_context(tc.psum_pool(name="ps_a", bufs=4))
+
+        ctx.enter_context(tc.manual_schedule())
+
+        misc = const.tile([P, C + P], BF16, name="misc")
+        nc.vector.memset(misc[:], 0.0)
+        nc.scalar.dma_start(out=misc[0:1, 0:C], in_=out_b.rearrange("(o n) -> o n", o=1))
+        nc.scalar.dma_start(out=misc[0:8, C:C + P], in_=ada1_scale.rearrange("o (a p) i -> (o a) (p i)", p=P))
+        nc.scalar.dma_start(out=misc[8:16, C:C + P], in_=ada1_shift.rearrange("o (a p) i -> (o a) (p i)", p=P))
+        warm = const.tile([P, 2], F32, name="warm")
+        nc.vector.memset(warm[:, 0:1], 1.0)
+        nc.scalar.activation(out=warm[:, 1:2], in_=warm[:, 0:1], func=ACT.Sqrt)
+        ones_b = const.tile([P, P], BF16, name="ones_b")
+        nc.vector.memset(ones_b[:], 1.0)
+
+        a_raw = []
+        w_raw = []
+        x_raw = {}
+        for s in range(8):
+            a_raw.append(raw.tile([P, C], BF16, name="a_raw%d" % s))
+            w_raw.append(raw.tile([P, C], BF16, name="w_raw%d" % s))
+
+        def load_a(s):
+            nc.sync.dma_start(out=a_raw[s][:], in_=o_flat[P * s:P * (s + 1), :])
+
+        for s in range(4):
+            load_a(s)
+        for j in range(8):
+            nc.sync.dma_start(out=w_raw[j][:], in_=out_w[P * j:P * (j + 1), :])
+        for s in range(4, 8):
+            load_a(s)
+        order = [1, 2, 3, 4, 5, 6, 7, 0]
+        for a in order:
+            x_raw[a] = raw.tile([P, C], BF16, name="x_raw%d" % a)
+            nc.sync.dma_start(out=x_raw[a][:], in_=x_flat[P * a:P * (a + 1), :])
+
+        ident_f = const.tile([P, P], F32, name="ident_f")
+        make_identity(nc, ident_f[:])
+        perm_f = const.tile([P, P], F32, name="perm_f")
+        nc.vector.tensor_copy(
+            out=perm_f[:].rearrange("p (r w c) -> p w r c", r=8, w=2, c=8),
+            in_=ident_f[:].rearrange("p (w r c) -> p w r c", w=2, r=8, c=8),
+        )
+        ident_b = const.tile([P, P], BF16, name="ident_b")
+        nc.vector.tensor_copy(out=ident_b[:], in_=ident_f[:])
+
+        bias_bc = const.tile([P, C], BF16, name="bias_bc")
+        ada_f = const.tile([P, 16], F32, name="ada_f")
+
+        def small_prep():
+            for h in range(2):
+                pb = ps_t.tile([P, 512], F32, name="pb", tag="tp")
+                nc.tensor.matmul(pb[:], lhsT=ones_b[:], rhs=misc[:, 512 * h:512 * (h + 1)], start=True, stop=True)
+                nc.scalar.copy(out=bias_bc[:, 512 * h:512 * (h + 1)], in_=pb[:])
+            pa = ps_t.tile([P, P], BF16, name="pa", tag="tp")
+            nc.tensor.transpose(pa[:], misc[:, C:C + P], ident_b[:])
+            nc.vector.tensor_copy(out=ada_f[:], in_=pa[:, 0:16])
+
+        copy_eng = [nc.scalar.copy, nc.vector.tensor_copy]
+
+        a_state = {}
+
+        def a_turn(wi, s2, eng):
+            if s2 == 0:
+                a_state[wi] = agrp.tile([P, 2048], BF16, name="a_grp", align_bytes=64)
+            gw = a_state[wi][:].bitcast(F32).rearrange("p (q j u) -> p q j u", q=16, j=32, u=2)
+            words = a_raw[2 * wi + s2][:].bitcast(F32)
+            pt = ps_t.tile([P, 512], F32, name="pt", tag="tp")
+            for u in range(2):
+                for g in range(2):
+                    nc.tensor.transpose(
+                        pt[:, (2 * u + g) * P:(2 * u + g + 1) * P],
+                        words[:, 256 * g + u:256 * (g + 1):2],
+                        perm_f[:],
+                    )
+            pv = pt[:].rearrange("p (u q jj) -> p q jj u", u=2, q=16, jj=16)
+            cp = copy_eng[eng]
+            if s2 == 0:
+                cp(out=gw[:, :, 4:20, :], in_=pv)
+            else:
+                cp(out=gw[:, :, 20:32, :], in_=pv[:, :, 0:12, :])
+                cp(out=gw[:, :, 0:4, :], in_=pv[:, :, 12:16, :])
+
+        a_cs = {}
+
+        def a_quant(wi):
+            codes = agrp.tile([P, 512], U32, name="a_codes", align_bytes=64)
+            scales = agrp.tile([P, 512], U8, name="a_scales", align_bytes=64)
+            nc.vector.quantize_mx(out=codes[:].bitcast(FP8X4), scales=scales[:], in_=a_state[wi][:])
+            a_cs[wi] = (codes, scales)
+
+        w_grp = []
+        w_codes = []
+        w_scales = []
+        for h in range(2):
+            w_grp.append(const.tile([P, 4096], BF16, name="w_grp%d" % h, align_bytes=64))
+            w_codes.append(const.tile([P, 1024], U32, name="w_codes%d" % h, align_bytes=64))
+            w_scales.append(const.tile([P, 1024], U8, name="w_scales%d" % h, align_bytes=64))
+
+        def w_turn(j, eng):
+            h, jj = divmod(j, 4)
+            gw = w_grp[h][:].bitcast(F32).rearrange("p (g n u) -> p g n u", g=2, n=512, u=2)
+            words = w_raw[j][:].bitcast(F32)
+            pt = ps_t.tile([P, 512], F32, name="pt", tag="tp")
+            for g in range(2):
+                for u in range(2):
+                    nc.tensor.transpose(
+                        pt[:, (2 * g + u) * P:(2 * g + u + 1) * P],
+                        words[:, 256 * g + u:256 * (g + 1):2],
+                        ident_f[:],
+                    )
+            copy_eng[eng](
+                out=gw[:, :, P * jj:P * (jj + 1), :],
+                in_=pt[:].rearrange("p (g u n) -> p g n u", g=2, u=2, n=P),
+            )
+
+        def w_quant(h, q):
+            for g in range(2):
+                lo = 512 * g + 256 * q
+                nc.vector.quantize_mx(
+                    out=w_codes[h][:, lo:lo + 256].bitcast(FP8X4),
+                    scales=w_scales[h][:, lo:lo + 256],
+                    in_=w_grp[h][:, 4 * lo:4 * (lo + 256)],
+                )
+
+        accs = {}
+        sts = {}
+        ts = {}
+        xcs = {}
+        ys = {}
+
+        def mmh(k, h):
+            codes, scales = a_cs[k // 2]
+            acc = ps_a.tile([P, 512], F32, name="acc")
+            accs[(k, h)] = acc
+            for g in range(2):
+                lo = 256 * g + P * (k % 2)
+                nc.tensor.matmul_mx(
+                    out=acc[:],
+                    lhsT=codes[:, lo:lo + P].bitcast(FP8X4),
+                    lhsT_scale=scales[:, lo:lo + P],
+                    rhs=w_codes[h][:, 512 * g:512 * (g + 1)].bitcast(FP8X4),
+                    rhs_scale=w_scales[h][:, 512 * g:512 * (g + 1)],
+                    start=(g == 0),
+                    stop=(g == 1),
+                )
+
+        def mm(k):
+            mmh(k, 0)
+            mmh(k, 1)
+
+        def st_a(k, h):
+            if h == 0:
+                sts[k] = stat.tile([P, 16], F32, name="st")
+                ts[k] = work.tile([P, C], F32, name="t", bufs=4)
+            cols = slice(512 * h, 512 * (h + 1))
+            nc.vector.scalar_tensor_tensor(
+                out=ts[k][:, cols], in0=accs[(k, h)][:], scalar=1.0, in1=bias_bc[:, cols],
+                op0=ALU.mult, op1=ALU.add, accum_out=sts[k][:, h:h + 1],
+            )
+
+        def st_nm(k):
+            st = sts[k]
+            nc.gpsimd.tensor_scalar(out=st[:, 2:3], in0=st[:, 0:1], scalar1=st[:, 1:2], scalar2=-1.0 / C, op0=ALU.add, op1=ALU.mult)
+
+        def st_b(k):
+            st = sts[k]
+            junk = work.tile([P, C], F32, name="junk", bufs=2)
+            nc.scalar.activation(out=junk[:], in_=ts[k][:], func=ACT.Square, bias=st[:, 2:3], scale=1.0, accum_out=st[:, 3:4])
+            nc.scalar.activation(out=st[:, 4:5], in_=st[:, 3:4], func=ACT.Sqrt, scale=1.0 / (C - 1))
+            nc.scalar.activation(out=st[:, 5:6], in_=st[:, 4:5], func=ACT.Copy, bias=EPS, scale=1.0)
+
+        def st_rec(k):
+            st = sts[k]
+            a = order[k]
+            nc.vector.reciprocal(out=st[:, 6:7], in_=st[:, 5:6])
+            nc.gpsimd.tensor_scalar(out=st[:, 7:8], in0=st[:, 6:7], scalar1=ada_f[:, a:a + 1], scalar2=0.0, op0=ALU.mult, op1=ALU.add)
+            nc.gpsimd.tensor_scalar(out=st[:, 8:9], in0=st[:, 2:3], scalar1=st[:, 7:8], scalar2=ada_f[:, 8 + a:9 + a], op0=ALU.mult, op1=ALU.add)
+
+        def st_xc(k, on_vector):
+            a = order[k]
+            xc = work.tile([P, C], F32, name="xc", bufs=1)
+            xcs[k] = xc
+            if on_vector:
+                nc.vector.tensor_scalar(out=xc[:], in0=x_raw[a][:], scalar1=sts[k][:, 8:9], scalar2=None, op0=ALU.add)
+            else:
+                nc.gpsimd.tensor_scalar(out=xc[:], in0=x_raw[a][:], scalar1=1.0, scalar2=sts[k][:, 8:9], op0=ALU.mult, op1=ALU.add)
+
+        def st_d(k):
+            a = order[k]
+            y = work.tile([P, C], F32, name="y")
+            ys[k] = y
+            nc.vector.scalar_tensor_tensor(out=y[:], in0=ts[k][:], scalar=sts[k][:, 7:8], in1=xcs[k][:], op0=ALU.mult, op1=ALU.add)
+            nc.sync.dma_start(out=y_flat[P * a:P * (a + 1), :], in_=y[:])
+            yb = work.tile([P, C], FP8, name="yb")
+            nc.scalar.activation(out=yb[:], in_=y[:], func=ACT.Copy, scale=Y_SCALE, saturate=False)
+            nc.sync.dma_start(out=yb_flat[P * a:P * (a + 1), :], in_=yb[:].bitcast(U8))
+
+        a_turn(0, 0, 0)
+        a_turn(0, 1, 1)
+        a_turn(1, 0, 0)
+        a_quant(0)
+        a_turn(1, 1, 1)
+        w_turn(0, 0)
+        a_quant(1)
+        w_turn(1, 1)
+        small_prep()
+        w_quant(0, 0)
+        w_turn(2, 0)
+        w_turn(3, 1)
+        w_quant(0, 1)
+        w_turn(4, 0)
+        w_turn(5, 1)
+        mmh(0, 0)
+        mmh(1, 0)
+        st_a(0, 0)
+        w_quant(1, 0)
+        w_turn(6, 0)
+        st_a(1, 0)
+        w_turn(7, 1)
+        w_quant(1, 1)
+        mmh(0, 1)
+        mmh(1, 1)
+        st_a(0, 1)
+        st_nm(0)
+        st_b(0)
+        mm(2)
+        st_a(1, 1)
+        st_nm(1)
+        st_b(1)
+        a_turn(2, 0, 0)
+        mm(3)
+        a_turn(2, 1, 0)
+
+        for k in range(1, 10):
+            if k == 2:
+                a_turn(3, 0, 0)
+            if k == 3:
+                a_turn(3, 1, 0)
+            if k - 1 < 8:
+                st_rec(k - 1)
+            if 0 <= k - 2 < 8:
+                st_d(k - 2)
+            if k - 1 < 8:
+                st_xc(k - 1, k - 1 >= 6)
+            if k + 1 < 8:
+                st_a(k + 1, 0)
+                st_a(k + 1, 1)
+                st_nm(k + 1)
+                st_b(k + 1)
+            if k == 2:
+                a_quant(2)
+            if k == 4:
+                a_quant(3)
+            if k >= 2 and k + 2 < 8:
+                mm(k + 2)

@@ -48,6 +48,15 @@ def tile_swintransformerblock_pb_kernel(tc, o_attn, out_w, out_b, ada1_scale, ad
         nc.scalar.activation(out=warm[:, 1:2], in_=warm[:, 0:1], func=ACT.Sqrt)
         ones_b = const.tile([P, P], BF16, name="ones_b")
         nc.vector.memset(ones_b[:], 1.0)
+        zeros_b = const.tile([P, 512], BF16, name="zeros_b")
+        nc.vector.memset(zeros_b[:], 0.0)
+
+        def keep_warm(n):
+            pd = ps_t.tile([P, 512], F32, name="pd", tag="tp")
+            for i in range(n):
+                nc.tensor.matmul(pd[:], lhsT=ones_b[:], rhs=zeros_b[:], start=True, stop=True)
+
+        keep_warm(4)
 
         a_raw = []
         w_raw = []
@@ -197,7 +206,7 @@ def tile_swintransformerblock_pb_kernel(tc, o_attn, out_w, out_b, ada1_scale, ad
 
         def st_nm(k):
             st = sts[k]
-            nc.gpsimd.tensor_scalar(out=st[:, 2:3], in0=st[:, 0:1], scalar1=st[:, 1:2], scalar2=-1.0 / C, op0=ALU.add, op1=ALU.mult)
+            nc.vector.tensor_scalar(out=st[:, 2:3], in0=st[:, 0:1], scalar1=st[:, 1:2], scalar2=-1.0 / C, op0=ALU.add, op1=ALU.mult)
 
         def st_b(k):
             st = sts[k]
@@ -207,11 +216,16 @@ def tile_swintransformerblock_pb_kernel(tc, o_attn, out_w, out_b, ada1_scale, ad
             nc.scalar.activation(out=st[:, 5:6], in_=st[:, 4:5], func=ACT.Copy, bias=EPS, scale=1.0)
 
         def st_rec(k):
+            nc.vector.reciprocal(out=sts[k][:, 6:7], in_=sts[k][:, 5:6])
+
+        def st_r(k):
+            a = order[k]
+            nc.vector.tensor_scalar(out=sts[k][:, 7:8], in0=sts[k][:, 6:7], scalar1=ada_f[:, a:a + 1], scalar2=None, op0=ALU.mult)
+
+        def st_c(k):
             st = sts[k]
             a = order[k]
-            nc.vector.reciprocal(out=st[:, 6:7], in_=st[:, 5:6])
-            nc.gpsimd.tensor_scalar(out=st[:, 7:8], in0=st[:, 6:7], scalar1=ada_f[:, a:a + 1], scalar2=0.0, op0=ALU.mult, op1=ALU.add)
-            nc.gpsimd.tensor_scalar(out=st[:, 8:9], in0=st[:, 2:3], scalar1=st[:, 7:8], scalar2=ada_f[:, 8 + a:9 + a], op0=ALU.mult, op1=ALU.add)
+            nc.vector.tensor_scalar(out=st[:, 8:9], in0=st[:, 2:3], scalar1=st[:, 7:8], scalar2=ada_f[:, 8 + a:9 + a], op0=ALU.mult, op1=ALU.add)
 
         def st_xc(k, on_vector):
             a = order[k]
@@ -222,25 +236,55 @@ def tile_swintransformerblock_pb_kernel(tc, o_attn, out_w, out_b, ada1_scale, ad
             else:
                 nc.gpsimd.tensor_scalar(out=xc[:], in0=x_raw[a][:], scalar1=1.0, scalar2=sts[k][:, 8:9], op0=ALU.mult, op1=ALU.add)
 
-        def st_d(k):
+        ybs = {}
+
+        def st_d(k, h):
+            if h == 0:
+                ys[k] = work.tile([P, C], F32, name="y")
+                ybs[k] = work.tile([P, C], FP8, name="yb")
+            cols = slice(512 * h, 512 * (h + 1))
+            nc.vector.scalar_tensor_tensor(out=ys[k][:, cols], in0=ts[k][:, cols], scalar=sts[k][:, 7:8], in1=xcs[k][:, cols], op0=ALU.mult, op1=ALU.add)
+
+        def st_out(k, lo, hi, on_vector):
             a = order[k]
-            y = work.tile([P, C], F32, name="y")
-            ys[k] = y
-            nc.vector.scalar_tensor_tensor(out=y[:], in0=ts[k][:], scalar=sts[k][:, 7:8], in1=xcs[k][:], op0=ALU.mult, op1=ALU.add)
-            nc.sync.dma_start(out=y_flat[P * a:P * (a + 1), :], in_=y[:])
-            yb = work.tile([P, C], FP8, name="yb")
-            nc.scalar.activation(out=yb[:], in_=y[:], func=ACT.Copy, scale=Y_SCALE, saturate=False)
-            nc.sync.dma_start(out=yb_flat[P * a:P * (a + 1), :], in_=yb[:].bitcast(U8))
+            rows = slice(P * a, P * (a + 1))
+            nc.sync.dma_start(out=y_flat[rows, lo:hi], in_=ys[k][:, lo:hi])
+            if on_vector:
+                nc.vector.tensor_scalar(out=ybs[k][:, lo:hi], in0=ys[k][:, lo:hi], scalar1=Y_SCALE, scalar2=None, op0=ALU.mult, saturate=False)
+            else:
+                nc.scalar.activation(out=ybs[k][:, lo:hi], in_=ys[k][:, lo:hi], func=ACT.Copy, scale=Y_SCALE, saturate=False)
+            nc.sync.dma_start(out=yb_flat[rows, lo:hi], in_=ybs[k][:, lo:hi].bitcast(U8))
+
+        def w_quant_one(j, g):
+            h, jj = divmod(j, 4)
+            lo = 512 * g + P * jj
+            nc.vector.quantize_mx(
+                out=w_codes[h][:, lo:lo + P].bitcast(FP8X4),
+                scales=w_scales[h][:, lo:lo + P],
+                in_=w_grp[h][:, 4 * lo:4 * (lo + P)],
+            )
+
+        def w_turn_last(j):
+            h, jj = divmod(j, 4)
+            gw = w_grp[h][:].bitcast(F32).rearrange("p (g n u) -> p g n u", g=2, n=512, u=2)
+            words = w_raw[j][:].bitcast(F32)
+            for g in range(2):
+                pt = ps_t.tile([P, 256], F32, name="pt", tag="tp")
+                for u in range(2):
+                    nc.tensor.transpose(pt[:, u * P:(u + 1) * P], words[:, 256 * g + u:256 * (g + 1):2], ident_f[:])
+                copy_eng[g](out=gw[:, g, P * jj:P * (jj + 1), :], in_=pt[:].rearrange("p (u n) -> p n u", u=2, n=P))
 
         a_turn(0, 0, 0)
         a_turn(0, 1, 1)
+        small_prep()
         a_turn(1, 0, 0)
         a_quant(0)
         a_turn(1, 1, 1)
+        keep_warm(1)
         w_turn(0, 0)
         a_quant(1)
         w_turn(1, 1)
-        small_prep()
+        keep_warm(1)
         w_quant(0, 0)
         w_turn(2, 0)
         w_turn(3, 1)
@@ -253,8 +297,11 @@ def tile_swintransformerblock_pb_kernel(tc, o_attn, out_w, out_b, ada1_scale, ad
         w_quant(1, 0)
         w_turn(6, 0)
         st_a(1, 0)
-        w_turn(7, 1)
-        w_quant(1, 1)
+        w_quant_one(6, 0)
+        w_quant_one(6, 1)
+        w_turn_last(7)
+        w_quant_one(7, 0)
+        w_quant_one(7, 1)
         mmh(0, 1)
         mmh(1, 1)
         st_a(0, 1)
@@ -269,24 +316,38 @@ def tile_swintransformerblock_pb_kernel(tc, o_attn, out_w, out_b, ada1_scale, ad
         a_turn(2, 1, 0)
 
         for k in range(1, 10):
+            kr = k - 1
+            kd = k - 2
+            ka = k + 1
             if k == 2:
                 a_turn(3, 0, 0)
             if k == 3:
                 a_turn(3, 1, 0)
-            if k - 1 < 8:
-                st_rec(k - 1)
-            if 0 <= k - 2 < 8:
-                st_d(k - 2)
-            if k - 1 < 8:
-                st_xc(k - 1, k - 1 >= 6)
-            if k + 1 < 8:
-                st_a(k + 1, 0)
-                st_a(k + 1, 1)
-                st_nm(k + 1)
-                st_b(k + 1)
+            if kr < 8:
+                st_rec(kr)
+            if kd >= 0:
+                st_d(kd, 0)
+                if kd == 7:
+                    st_out(kd, 0, 512, False)
+            if kr < 8:
+                st_r(kr)
+            if kd >= 0:
+                st_d(kd, 1)
+                if kd == 7:
+                    st_out(kd, 512, C, True)
+                else:
+                    st_out(kd, 0, C, False)
             if k == 2:
                 a_quant(2)
             if k == 4:
                 a_quant(3)
+            if kr < 8:
+                st_c(kr)
+                st_xc(kr, kr >= 6)
             if k >= 2 and k + 2 < 8:
                 mm(k + 2)
+            if ka < 8:
+                st_a(ka, 0)
+                st_a(ka, 1)
+                st_nm(ka)
+                st_b(ka)

@@ -48,15 +48,6 @@ def tile_swintransformerblock_pb_kernel(tc, o_attn, out_w, out_b, ada1_scale, ad
         nc.scalar.activation(out=warm[:, 1:2], in_=warm[:, 0:1], func=ACT.Sqrt)
         ones_b = const.tile([P, P], BF16, name="ones_b")
         nc.vector.memset(ones_b[:], 1.0)
-        zeros_b = const.tile([P, 512], BF16, name="zeros_b")
-        nc.vector.memset(zeros_b[:], 0.0)
-
-        def keep_warm(n):
-            pd = ps_t.tile([P, 512], F32, name="pd", tag="tp")
-            for i in range(n):
-                nc.tensor.matmul(pd[:], lhsT=ones_b[:], rhs=zeros_b[:], start=True, stop=True)
-
-        keep_warm(4)
 
         a_raw = []
         w_raw = []
@@ -68,11 +59,11 @@ def tile_swintransformerblock_pb_kernel(tc, o_attn, out_w, out_b, ada1_scale, ad
         def load_a(s):
             nc.sync.dma_start(out=a_raw[s][:], in_=o_flat[P * s:P * (s + 1), :])
 
-        for s in range(4):
+        for s in range(2):
             load_a(s)
         for j in range(8):
             nc.sync.dma_start(out=w_raw[j][:], in_=out_w[P * j:P * (j + 1), :])
-        for s in range(4, 8):
+        for s in range(2, 8):
             load_a(s)
         order = [1, 2, 3, 4, 5, 6, 7, 0]
         for a in order:
@@ -105,12 +96,12 @@ def tile_swintransformerblock_pb_kernel(tc, o_attn, out_w, out_b, ada1_scale, ad
 
         a_state = {}
 
-        def a_turn(wi, s2, eng):
-            if s2 == 0:
-                a_state[wi] = agrp.tile([P, 2048], BF16, name="a_grp", align_bytes=64)
-            gw = a_state[wi][:].bitcast(F32).rearrange("p (q j u) -> p q j u", q=16, j=32, u=2)
+        a_bank = {}
+
+        def a_turn(wi, s2):
             words = a_raw[2 * wi + s2][:].bitcast(F32)
             pt = ps_t.tile([P, 512], F32, name="pt", tag="tp")
+            a_bank[(wi, s2)] = pt
             for u in range(2):
                 for g in range(2):
                     nc.tensor.transpose(
@@ -118,7 +109,12 @@ def tile_swintransformerblock_pb_kernel(tc, o_attn, out_w, out_b, ada1_scale, ad
                         words[:, 256 * g + u:256 * (g + 1):2],
                         perm_f[:],
                     )
-            pv = pt[:].rearrange("p (u q jj) -> p q jj u", u=2, q=16, jj=16)
+
+        def a_copy(wi, s2, eng):
+            if s2 == 0:
+                a_state[wi] = agrp.tile([P, 2048], BF16, name="a_grp", align_bytes=64)
+            gw = a_state[wi][:].bitcast(F32).rearrange("p (q j u) -> p q j u", q=16, j=32, u=2)
+            pv = a_bank[(wi, s2)][:].rearrange("p (u q jj) -> p q jj u", u=2, q=16, jj=16)
             cp = copy_eng[eng]
             if s2 == 0:
                 cp(out=gw[:, :, 4:20, :], in_=pv)
@@ -274,55 +270,57 @@ def tile_swintransformerblock_pb_kernel(tc, o_attn, out_w, out_b, ada1_scale, ad
                     nc.tensor.transpose(pt[:, u * P:(u + 1) * P], words[:, 256 * g + u:256 * (g + 1):2], ident_f[:])
                 copy_eng[g](out=gw[:, g, P * jj:P * (jj + 1), :], in_=pt[:].rearrange("p (u n) -> p n u", u=2, n=P))
 
-        a_turn(0, 0, 0)
-        a_turn(0, 1, 1)
+        a_turn(0, 0)
+        a_copy(0, 0, 0)
+        a_turn(0, 1)
+        a_copy(0, 1, 1)
         small_prep()
-        a_turn(1, 0, 0)
-        a_quant(0)
-        a_turn(1, 1, 1)
-        keep_warm(1)
         w_turn(0, 0)
-        a_quant(1)
+        a_quant(0)
         w_turn(1, 1)
-        keep_warm(1)
         w_quant(0, 0)
         w_turn(2, 0)
         w_turn(3, 1)
         w_quant(0, 1)
         w_turn(4, 0)
         w_turn(5, 1)
-        mmh(0, 0)
-        mmh(1, 0)
-        st_a(0, 0)
         w_quant(1, 0)
         w_turn(6, 0)
-        st_a(1, 0)
         w_quant_one(6, 0)
         w_quant_one(6, 1)
         w_turn_last(7)
         w_quant_one(7, 0)
         w_quant_one(7, 1)
+        a_turn(1, 0)
+        a_copy(1, 0, 0)
+        a_turn(1, 1)
+        a_copy(1, 1, 0)
+        mmh(0, 0)
         mmh(0, 1)
+        mmh(1, 0)
         mmh(1, 1)
+        st_a(0, 0)
         st_a(0, 1)
         st_nm(0)
         st_b(0)
-        mm(2)
+        a_quant(1)
+        a_turn(2, 0)
+        a_turn(2, 1)
+        st_a(1, 0)
         st_a(1, 1)
         st_nm(1)
         st_b(1)
-        a_turn(2, 0, 0)
+        mm(2)
         mm(3)
-        a_turn(2, 1, 0)
+        a_copy(2, 0, 0)
+        a_copy(2, 1, 0)
+        a_turn(3, 0)
+        a_turn(3, 1)
 
         for k in range(1, 10):
             kr = k - 1
             kd = k - 2
             ka = k + 1
-            if k == 2:
-                a_turn(3, 0, 0)
-            if k == 3:
-                a_turn(3, 1, 0)
             if kr < 8:
                 st_rec(kr)
             if kd >= 0:
@@ -351,3 +349,7 @@ def tile_swintransformerblock_pb_kernel(tc, o_attn, out_w, out_b, ada1_scale, ad
                 st_a(ka, 1)
                 st_nm(ka)
                 st_b(ka)
+            if k == 1:
+                a_copy(3, 0, 0)
+            if k == 2:
+                a_copy(3, 1, 0)

@@ -38,6 +38,13 @@ def tile_swintransformerblock_pb_kernel(tc, o_attn, out_w, out_b, ada1_scale, ad
 
         ctx.enter_context(tc.manual_schedule())
 
+        ones_b = const.tile([P, P], BF16, name="ones_b")
+        nc.vector.memset(ones_b[:], 1.0)
+        zeros_b = const.tile([P, 512], BF16, name="zeros_b")
+        nc.vector.memset(zeros_b[:], 0.0)
+        pd = ps_t.tile([P, 512], F32, name="pd", tag="tp")
+        for i in range(4):
+            nc.tensor.matmul(pd[:], lhsT=ones_b[:], rhs=zeros_b[:], start=True, stop=True)
         misc = const.tile([P, C + P], BF16, name="misc")
         nc.vector.memset(misc[:], 0.0)
         nc.scalar.dma_start(out=misc[0:1, 0:C], in_=out_b.rearrange("(o n) -> o n", o=1))
@@ -46,8 +53,6 @@ def tile_swintransformerblock_pb_kernel(tc, o_attn, out_w, out_b, ada1_scale, ad
         warm = const.tile([P, 2], F32, name="warm")
         nc.vector.memset(warm[:, 0:1], 1.0)
         nc.scalar.activation(out=warm[:, 1:2], in_=warm[:, 0:1], func=ACT.Sqrt)
-        ones_b = const.tile([P, P], BF16, name="ones_b")
-        nc.vector.memset(ones_b[:], 1.0)
 
         a_raw = []
         w_raw = []
@@ -90,25 +95,37 @@ def tile_swintransformerblock_pb_kernel(tc, o_attn, out_w, out_b, ada1_scale, ad
                 nc.scalar.copy(out=bias_bc[:, 512 * h:512 * (h + 1)], in_=pb[:])
             pa = ps_t.tile([P, P], BF16, name="pa", tag="tp")
             nc.tensor.transpose(pa[:], misc[:, C:C + P], ident_b[:])
-            nc.vector.tensor_copy(out=ada_f[:], in_=pa[:, 0:16])
+            nc.scalar.copy(out=ada_f[:], in_=pa[:, 0:16])
 
         copy_eng = [nc.scalar.copy, nc.vector.tensor_copy]
+
+        sorted_words = {}
+
+        def sort_words(key, src):
+            dst = raw.tile([P, 512], F32, name="sw_%s%d" % key)
+            nc.vector.tensor_copy(
+                out=dst[:].rearrange("p (g u q) -> p g u q", g=2, u=2, q=P),
+                in_=src[:].bitcast(F32).rearrange("p (g q u) -> p g u q", g=2, q=P, u=2),
+            )
+            sorted_words[key] = dst
+
+        def turn_src(key, src, g, u):
+            if key in sorted_words:
+                lo = 256 * g + P * u
+                return sorted_words[key][:, lo:lo + P]
+            return src[:].bitcast(F32)[:, 256 * g + u:256 * (g + 1):2]
 
         a_state = {}
 
         a_bank = {}
 
         def a_turn(wi, s2):
-            words = a_raw[2 * wi + s2][:].bitcast(F32)
+            s = 2 * wi + s2
             pt = ps_t.tile([P, 512], F32, name="pt", tag="tp")
             a_bank[(wi, s2)] = pt
             for u in range(2):
                 for g in range(2):
-                    nc.tensor.transpose(
-                        pt[:, (2 * u + g) * P:(2 * u + g + 1) * P],
-                        words[:, 256 * g + u:256 * (g + 1):2],
-                        perm_f[:],
-                    )
+                    nc.tensor.transpose(pt[:, (2 * u + g) * P:(2 * u + g + 1) * P], turn_src(("a", s), a_raw[s], g, u), perm_f[:])
 
         def a_copy(wi, s2, eng):
             if s2 == 0:
@@ -141,15 +158,10 @@ def tile_swintransformerblock_pb_kernel(tc, o_attn, out_w, out_b, ada1_scale, ad
         def w_turn(j, eng):
             h, jj = divmod(j, 4)
             gw = w_grp[h][:].bitcast(F32).rearrange("p (g n u) -> p g n u", g=2, n=512, u=2)
-            words = w_raw[j][:].bitcast(F32)
             pt = ps_t.tile([P, 512], F32, name="pt", tag="tp")
             for g in range(2):
                 for u in range(2):
-                    nc.tensor.transpose(
-                        pt[:, (2 * g + u) * P:(2 * g + u + 1) * P],
-                        words[:, 256 * g + u:256 * (g + 1):2],
-                        ident_f[:],
-                    )
+                    nc.tensor.transpose(pt[:, (2 * g + u) * P:(2 * g + u + 1) * P], turn_src(("w", j), w_raw[j], g, u), ident_f[:])
             copy_eng[eng](
                 out=gw[:, :, P * jj:P * (jj + 1), :],
                 in_=pt[:].rearrange("p (g u n) -> p g n u", g=2, u=2, n=P),
@@ -270,31 +282,31 @@ def tile_swintransformerblock_pb_kernel(tc, o_attn, out_w, out_b, ada1_scale, ad
                     nc.tensor.transpose(pt[:, u * P:(u + 1) * P], words[:, 256 * g + u:256 * (g + 1):2], ident_f[:])
                 copy_eng[g](out=gw[:, g, P * jj:P * (jj + 1), :], in_=pt[:].rearrange("p (u n) -> p n u", u=2, n=P))
 
-        a_turn(0, 0)
-        a_copy(0, 0, 0)
-        a_turn(0, 1)
-        a_copy(0, 1, 1)
-        small_prep()
-        w_turn(0, 0)
-        a_quant(0)
-        w_turn(1, 1)
-        w_quant(0, 0)
-        w_turn(2, 0)
-        w_turn(3, 1)
-        w_quant(0, 1)
-        w_turn(4, 0)
-        w_turn(5, 1)
-        w_quant(1, 0)
-        w_turn(6, 0)
-        w_quant_one(6, 0)
-        w_quant_one(6, 1)
-        w_turn_last(7)
-        w_quant_one(7, 0)
-        w_quant_one(7, 1)
-        a_turn(1, 0)
-        a_copy(1, 0, 0)
-        a_turn(1, 1)
-        a_copy(1, 1, 0)
+        first = [("a", 0), ("a", 1)] + [("w", j) for j in range(8)] + [("a", 2), ("a", 3)]
+
+        def sort_ahead(i):
+            if i < len(first):
+                kind, s = first[i]
+                sort_words(first[i], a_raw[s] if kind == "a" else w_raw[s])
+
+        for i in range(3):
+            sort_ahead(i)
+        for i in range(len(first)):
+            kind, s = first[i]
+            sort_ahead(i + 3)
+            if kind == "a":
+                a_turn(s // 2, s % 2)
+                a_copy(s // 2, s % 2, 0)
+            else:
+                w_turn(s, 0)
+            if first[i] == ("a", 1):
+                small_prep()
+            if first[i] == ("w", 0):
+                a_quant(0)
+            if kind == "w" and s in (2, 4, 6):
+                w_quant((s - 2) // 4, ((s - 2) // 2) % 2)
+            if first[i] == ("w", 7):
+                w_quant(1, 1)
         mmh(0, 0)
         mmh(0, 1)
         mmh(1, 0)

@@ -19,6 +19,10 @@ C = 1024
 EPS = 1e-5
 Y_SCALE = 150.0
 
+SORTED = ("w0", "w1", "w2", "w3", "w4", "w5", "w6", "a2", "a3")
+COPY_IN_ROUND = {0: (5,), 1: (6, 7)}
+QUANT_IN_ROUND = {2: 2, 3: 3}
+
 
 def tile_swintransformerblock_pb_kernel(tc, o_attn, out_w, out_b, ada1_scale, ada1_shift, x, out_0, out_1):
     nc = tc.nc
@@ -30,14 +34,19 @@ def tile_swintransformerblock_pb_kernel(tc, o_attn, out_w, out_b, ada1_scale, ad
     with ExitStack() as ctx:
         const = ctx.enter_context(tc.tile_pool(name="const", bufs=1))
         raw = ctx.enter_context(tc.tile_pool(name="raw", bufs=1))
-        agrp = ctx.enter_context(tc.tile_pool(name="agrp", bufs=2))
+        agrp = ctx.enter_context(tc.tile_pool(name="agrp", bufs=4))
         work = ctx.enter_context(tc.tile_pool(name="work", bufs=3))
-        stat = ctx.enter_context(tc.tile_pool(name="stat", bufs=6))
+        stat = ctx.enter_context(tc.tile_pool(name="stat", bufs=8))
         ps_t = ctx.enter_context(tc.psum_pool(name="ps_t", bufs=4))
         ps_a = ctx.enter_context(tc.psum_pool(name="ps_a", bufs=4))
 
         ctx.enter_context(tc.manual_schedule())
 
+        misc = const.tile([P, C + P], BF16, name="misc")
+        nc.vector.memset(misc[:], 0.0)
+        nc.scalar.dma_start(out=misc[0:1, 0:C], in_=out_b.rearrange("(o n) -> o n", o=1))
+        nc.scalar.dma_start(out=misc[0:8, C:C + P], in_=ada1_scale.rearrange("o (a p) i -> (o a) (p i)", p=P))
+        nc.scalar.dma_start(out=misc[8:16, C:C + P], in_=ada1_shift.rearrange("o (a p) i -> (o a) (p i)", p=P))
         ones_b = const.tile([P, P], BF16, name="ones_b")
         nc.vector.memset(ones_b[:], 1.0)
         zeros_b = const.tile([P, 512], BF16, name="zeros_b")
@@ -45,11 +54,6 @@ def tile_swintransformerblock_pb_kernel(tc, o_attn, out_w, out_b, ada1_scale, ad
         pd = ps_t.tile([P, 512], F32, name="pd", tag="tp")
         for i in range(4):
             nc.tensor.matmul(pd[:], lhsT=ones_b[:], rhs=zeros_b[:], start=True, stop=True)
-        misc = const.tile([P, C + P], BF16, name="misc")
-        nc.vector.memset(misc[:], 0.0)
-        nc.scalar.dma_start(out=misc[0:1, 0:C], in_=out_b.rearrange("(o n) -> o n", o=1))
-        nc.scalar.dma_start(out=misc[0:8, C:C + P], in_=ada1_scale.rearrange("o (a p) i -> (o a) (p i)", p=P))
-        nc.scalar.dma_start(out=misc[8:16, C:C + P], in_=ada1_shift.rearrange("o (a p) i -> (o a) (p i)", p=P))
         warm = const.tile([P, 2], F32, name="warm")
         nc.vector.memset(warm[:, 0:1], 1.0)
         nc.scalar.activation(out=warm[:, 1:2], in_=warm[:, 0:1], func=ACT.Sqrt)
@@ -87,22 +91,34 @@ def tile_swintransformerblock_pb_kernel(tc, o_attn, out_w, out_b, ada1_scale, ad
 
         bias_bc = const.tile([P, C], BF16, name="bias_bc")
         ada_f = const.tile([P, 16], F32, name="ada_f")
+        ig = const.tile([P, 16], F32, name="ig")
 
-        def small_prep():
+        def bias_mm():
+            pb = ps_a.tile([P, C], BF16, name="pb", tag="acc")
             for h in range(2):
-                pb = ps_t.tile([P, 512], F32, name="pb", tag="tp")
-                nc.tensor.matmul(pb[:], lhsT=ones_b[:], rhs=misc[:, 512 * h:512 * (h + 1)], start=True, stop=True)
-                nc.scalar.copy(out=bias_bc[:, 512 * h:512 * (h + 1)], in_=pb[:])
+                nc.tensor.matmul(pb[:, 512 * h:512 * (h + 1)], lhsT=ones_b[:], rhs=misc[:, 512 * h:512 * (h + 1)], start=True, stop=True)
+            return pb
+
+        def bias_copy(pb):
+            for h in range(2):
+                nc.scalar.copy(out=bias_bc[:, 512 * h:512 * (h + 1)], in_=pb[:, 512 * h:512 * (h + 1)])
+
+        def ada_prep():
             pa = ps_t.tile([P, P], BF16, name="pa", tag="tp")
             nc.tensor.transpose(pa[:], misc[:, C:C + P], ident_b[:])
             nc.scalar.copy(out=ada_f[:], in_=pa[:, 0:16])
 
-        copy_eng = [nc.scalar.copy, nc.vector.tensor_copy]
+        def ig_prep():
+            nc.vector.reciprocal(out=ig[:, 0:8], in_=ada_f[:, 0:8])
+            nc.vector.tensor_scalar(out=ig[:, 8:16], in0=ig[:, 0:8], scalar1=EPS, scalar2=None, op0=ALU.mult)
 
         sorted_words = {}
 
-        def sort_words(key, src):
-            dst = raw.tile([P, 512], F32, name="sw_%s%d" % key)
+        def sort_words(key):
+            if key not in SORTED:
+                return
+            src = a_raw[int(key[1])] if key[0] == "a" else w_raw[int(key[1])]
+            dst = raw.tile([P, 512], F32, name="sw_%s" % key)
             nc.vector.tensor_copy(
                 out=dst[:].rearrange("p (g u q) -> p g u q", g=2, u=2, q=P),
                 in_=src[:].bitcast(F32).rearrange("p (g q u) -> p g u q", g=2, q=P, u=2),
@@ -116,28 +132,26 @@ def tile_swintransformerblock_pb_kernel(tc, o_attn, out_w, out_b, ada1_scale, ad
             return src[:].bitcast(F32)[:, 256 * g + u:256 * (g + 1):2]
 
         a_state = {}
-
         a_bank = {}
 
-        def a_turn(wi, s2):
-            s = 2 * wi + s2
+        def a_turn(s):
             pt = ps_t.tile([P, 512], F32, name="pt", tag="tp")
-            a_bank[(wi, s2)] = pt
+            a_bank[s] = pt
             for u in range(2):
                 for g in range(2):
-                    nc.tensor.transpose(pt[:, (2 * u + g) * P:(2 * u + g + 1) * P], turn_src(("a", s), a_raw[s], g, u), perm_f[:])
+                    nc.tensor.transpose(pt[:, (2 * u + g) * P:(2 * u + g + 1) * P], turn_src("a%d" % s, a_raw[s], g, u), perm_f[:])
 
-        def a_copy(wi, s2, eng):
+        def a_copy(s):
+            wi, s2 = divmod(s, 2)
             if s2 == 0:
                 a_state[wi] = agrp.tile([P, 2048], BF16, name="a_grp", align_bytes=64)
             gw = a_state[wi][:].bitcast(F32).rearrange("p (q j u) -> p q j u", q=16, j=32, u=2)
-            pv = a_bank[(wi, s2)][:].rearrange("p (u q jj) -> p q jj u", u=2, q=16, jj=16)
-            cp = copy_eng[eng]
+            pv = a_bank[s][:].rearrange("p (u q jj) -> p q jj u", u=2, q=16, jj=16)
             if s2 == 0:
-                cp(out=gw[:, :, 4:20, :], in_=pv)
+                nc.scalar.copy(out=gw[:, :, 4:20, :], in_=pv)
             else:
-                cp(out=gw[:, :, 20:32, :], in_=pv[:, :, 0:12, :])
-                cp(out=gw[:, :, 0:4, :], in_=pv[:, :, 12:16, :])
+                nc.scalar.copy(out=gw[:, :, 20:32, :], in_=pv[:, :, 0:12, :])
+                nc.scalar.copy(out=gw[:, :, 0:4, :], in_=pv[:, :, 12:16, :])
 
         a_cs = {}
 
@@ -155,25 +169,26 @@ def tile_swintransformerblock_pb_kernel(tc, o_attn, out_w, out_b, ada1_scale, ad
             w_codes.append(const.tile([P, 1024], U32, name="w_codes%d" % h, align_bytes=64))
             w_scales.append(const.tile([P, 1024], U8, name="w_scales%d" % h, align_bytes=64))
 
-        def w_turn(j, eng):
+        def w_turn_copy(j):
             h, jj = divmod(j, 4)
-            gw = w_grp[h][:].bitcast(F32).rearrange("p (g n u) -> p g n u", g=2, n=512, u=2)
             pt = ps_t.tile([P, 512], F32, name="pt", tag="tp")
             for g in range(2):
                 for u in range(2):
-                    nc.tensor.transpose(pt[:, (2 * g + u) * P:(2 * g + u + 1) * P], turn_src(("w", j), w_raw[j], g, u), ident_f[:])
-            copy_eng[eng](
+                    nc.tensor.transpose(pt[:, (2 * g + u) * P:(2 * g + u + 1) * P], turn_src("w%d" % j, w_raw[j], g, u), ident_f[:])
+            gw = w_grp[h][:].bitcast(F32).rearrange("p (g n u) -> p g n u", g=2, n=512, u=2)
+            nc.scalar.copy(
                 out=gw[:, :, P * jj:P * (jj + 1), :],
                 in_=pt[:].rearrange("p (g u n) -> p g n u", g=2, u=2, n=P),
             )
 
-        def w_quant(h, q):
+        def w_quant(j0, n):
+            h, jj = divmod(j0, 4)
             for g in range(2):
-                lo = 512 * g + 256 * q
+                lo = 512 * g + P * jj
                 nc.vector.quantize_mx(
-                    out=w_codes[h][:, lo:lo + 256].bitcast(FP8X4),
-                    scales=w_scales[h][:, lo:lo + 256],
-                    in_=w_grp[h][:, 4 * lo:4 * (lo + 256)],
+                    out=w_codes[h][:, lo:lo + P * n].bitcast(FP8X4),
+                    scales=w_scales[h][:, lo:lo + P * n],
+                    in_=w_grp[h][:, 4 * lo:4 * (lo + P * n)],
                 )
 
         accs = {}
@@ -181,6 +196,7 @@ def tile_swintransformerblock_pb_kernel(tc, o_attn, out_w, out_b, ada1_scale, ad
         ts = {}
         xcs = {}
         ys = {}
+        ybs = {}
 
         def mmh(k, h):
             codes, scales = a_cs[k // 2]
@@ -202,166 +218,158 @@ def tile_swintransformerblock_pb_kernel(tc, o_attn, out_w, out_b, ada1_scale, ad
             mmh(k, 0)
             mmh(k, 1)
 
-        def st_a(k, h):
+        def p1(k, h):
             if h == 0:
                 sts[k] = stat.tile([P, 16], F32, name="st")
-                ts[k] = work.tile([P, C], F32, name="t", bufs=4)
+                ts[k] = work.tile([P, C], F32, name="t", bufs=6)
             cols = slice(512 * h, 512 * (h + 1))
             nc.vector.scalar_tensor_tensor(
                 out=ts[k][:, cols], in0=accs[(k, h)][:], scalar=1.0, in1=bias_bc[:, cols],
                 op0=ALU.mult, op1=ALU.add, accum_out=sts[k][:, h:h + 1],
             )
 
-        def st_nm(k):
+        def nm(k):
             st = sts[k]
             nc.vector.tensor_scalar(out=st[:, 2:3], in0=st[:, 0:1], scalar1=st[:, 1:2], scalar2=-1.0 / C, op0=ALU.add, op1=ALU.mult)
 
-        def st_b(k):
+        def p2(k):
             st = sts[k]
             junk = work.tile([P, C], F32, name="junk", bufs=2)
             nc.scalar.activation(out=junk[:], in_=ts[k][:], func=ACT.Square, bias=st[:, 2:3], scale=1.0, accum_out=st[:, 3:4])
+
+        def sq(k):
+            st = sts[k]
             nc.scalar.activation(out=st[:, 4:5], in_=st[:, 3:4], func=ACT.Sqrt, scale=1.0 / (C - 1))
-            nc.scalar.activation(out=st[:, 5:6], in_=st[:, 4:5], func=ACT.Copy, bias=EPS, scale=1.0)
 
-        def st_rec(k):
-            nc.vector.reciprocal(out=sts[k][:, 6:7], in_=sts[k][:, 5:6])
-
-        def st_r(k):
+        def dd(k):
+            st = sts[k]
             a = order[k]
-            nc.vector.tensor_scalar(out=sts[k][:, 7:8], in0=sts[k][:, 6:7], scalar1=ada_f[:, a:a + 1], scalar2=None, op0=ALU.mult)
+            nc.scalar.activation(out=st[:, 5:6], in_=st[:, 4:5], func=ACT.Identity, scale=ig[:, a:a + 1], bias=ig[:, 8 + a:9 + a])
 
-        def st_c(k):
+        def rec(k):
+            nc.vector.reciprocal(out=sts[k][:, 7:8], in_=sts[k][:, 5:6])
+
+        def cc(k):
             st = sts[k]
             a = order[k]
             nc.vector.tensor_scalar(out=st[:, 8:9], in0=st[:, 2:3], scalar1=st[:, 7:8], scalar2=ada_f[:, 8 + a:9 + a], op0=ALU.mult, op1=ALU.add)
 
-        def st_xc(k, on_vector):
+        def p3(k):
             a = order[k]
-            xc = work.tile([P, C], F32, name="xc", bufs=1)
+            xc = work.tile([P, C], F32, name="xc", bufs=2)
             xcs[k] = xc
-            if on_vector:
-                nc.vector.tensor_scalar(out=xc[:], in0=x_raw[a][:], scalar1=sts[k][:, 8:9], scalar2=None, op0=ALU.add)
-            else:
-                nc.gpsimd.tensor_scalar(out=xc[:], in0=x_raw[a][:], scalar1=1.0, scalar2=sts[k][:, 8:9], op0=ALU.mult, op1=ALU.add)
+            nc.gpsimd.tensor_scalar(out=xc[:], in0=x_raw[a][:], scalar1=1.0, scalar2=sts[k][:, 8:9], op0=ALU.mult, op1=ALU.add)
 
-        ybs = {}
-
-        def st_d(k, h):
+        def p4(k, h):
             if h == 0:
                 ys[k] = work.tile([P, C], F32, name="y")
-                ybs[k] = work.tile([P, C], FP8, name="yb")
+                ybs[k] = work.tile([P, C], FP8, name="yb", bufs=4)
             cols = slice(512 * h, 512 * (h + 1))
             nc.vector.scalar_tensor_tensor(out=ys[k][:, cols], in0=ts[k][:, cols], scalar=sts[k][:, 7:8], in1=xcs[k][:, cols], op0=ALU.mult, op1=ALU.add)
 
-        def st_out(k, lo, hi, on_vector):
+        def st0(k, lo, hi):
             a = order[k]
-            rows = slice(P * a, P * (a + 1))
-            nc.sync.dma_start(out=y_flat[rows, lo:hi], in_=ys[k][:, lo:hi])
+            nc.sync.dma_start(out=y_flat[P * a:P * (a + 1), lo:hi], in_=ys[k][:, lo:hi])
+
+        def p5(k, lo, hi, on_vector):
             if on_vector:
                 nc.vector.tensor_scalar(out=ybs[k][:, lo:hi], in0=ys[k][:, lo:hi], scalar1=Y_SCALE, scalar2=None, op0=ALU.mult, saturate=False)
             else:
                 nc.scalar.activation(out=ybs[k][:, lo:hi], in_=ys[k][:, lo:hi], func=ACT.Copy, scale=Y_SCALE, saturate=False)
-            nc.sync.dma_start(out=yb_flat[rows, lo:hi], in_=ybs[k][:, lo:hi].bitcast(U8))
 
-        def w_quant_one(j, g):
-            h, jj = divmod(j, 4)
-            lo = 512 * g + P * jj
-            nc.vector.quantize_mx(
-                out=w_codes[h][:, lo:lo + P].bitcast(FP8X4),
-                scales=w_scales[h][:, lo:lo + P],
-                in_=w_grp[h][:, 4 * lo:4 * (lo + P)],
-            )
+        def st1(k, lo, hi):
+            a = order[k]
+            nc.sync.dma_start(out=yb_flat[P * a:P * (a + 1), lo:hi], in_=ybs[k][:, lo:hi].bitcast(U8))
 
-        def w_turn_last(j):
-            h, jj = divmod(j, 4)
-            gw = w_grp[h][:].bitcast(F32).rearrange("p (g n u) -> p g n u", g=2, n=512, u=2)
-            words = w_raw[j][:].bitcast(F32)
-            for g in range(2):
-                pt = ps_t.tile([P, 256], F32, name="pt", tag="tp")
-                for u in range(2):
-                    nc.tensor.transpose(pt[:, u * P:(u + 1) * P], words[:, 256 * g + u:256 * (g + 1):2], ident_f[:])
-                copy_eng[g](out=gw[:, g, P * jj:P * (jj + 1), :], in_=pt[:].rearrange("p (u n) -> p n u", u=2, n=P))
-
-        first = [("a", 0), ("a", 1)] + [("w", j) for j in range(8)] + [("a", 2), ("a", 3)]
-
-        def sort_ahead(i):
-            if i < len(first):
-                kind, s = first[i]
-                sort_words(first[i], a_raw[s] if kind == "a" else w_raw[s])
-
-        for i in range(3):
-            sort_ahead(i)
-        for i in range(len(first)):
-            kind, s = first[i]
-            sort_ahead(i + 3)
-            if kind == "a":
-                a_turn(s // 2, s % 2)
-                a_copy(s // 2, s % 2, 0)
-            else:
-                w_turn(s, 0)
-            if first[i] == ("a", 1):
-                small_prep()
-            if first[i] == ("w", 0):
+        a_turn(0)
+        a_copy(0)
+        a_turn(1)
+        a_copy(1)
+        ada_prep()
+        for j in range(8):
+            sort_words("w%d" % j)
+            w_turn_copy(j)
+            if j == 3:
                 a_quant(0)
-            if kind == "w" and s in (2, 4, 6):
-                w_quant((s - 2) // 4, ((s - 2) // 2) % 2)
-            if first[i] == ("w", 7):
-                w_quant(1, 1)
+            if j == 5:
+                w_quant(0, 2)
+            if j == 6:
+                w_quant(2, 2)
+        sort_words("a2")
+        sort_words("a3")
+        w_quant(4, 2)
+        pb = bias_mm()
+        w_quant(6, 1)
+        w_quant(7, 1)
         mmh(0, 0)
+        bias_copy(pb)
+        a_turn(2)
+        a_copy(2)
         mmh(0, 1)
+        a_turn(3)
+        a_copy(3)
         mmh(1, 0)
         mmh(1, 1)
-        st_a(0, 0)
-        st_a(0, 1)
-        st_nm(0)
-        st_b(0)
+        p1(0, 0)
+        p1(0, 1)
+        nm(0)
+        p2(0)
+        ig_prep()
+        p1(1, 0)
         a_quant(1)
-        a_turn(2, 0)
-        a_turn(2, 1)
-        st_a(1, 0)
-        st_a(1, 1)
-        st_nm(1)
-        st_b(1)
+        a_turn(4)
+        sq(0)
+        dd(0)
+        a_copy(4)
+        p1(1, 1)
         mm(2)
+        a_turn(5)
         mm(3)
-        a_copy(2, 0, 0)
-        a_copy(2, 1, 0)
-        a_turn(3, 0)
-        a_turn(3, 1)
+        a_turn(6)
+        a_turn(7)
 
-        for k in range(1, 10):
-            kr = k - 1
+        for k in range(10):
+            kn = k + 1
             kd = k - 2
-            ka = k + 1
-            if kr < 8:
-                st_rec(kr)
-            if kd >= 0:
-                st_d(kd, 0)
-                if kd == 7:
-                    st_out(kd, 0, 512, False)
-            if kr < 8:
-                st_r(kr)
-            if kd >= 0:
-                st_d(kd, 1)
-                if kd == 7:
-                    st_out(kd, 512, C, True)
+            ka = k + 2
+            last = kd == 7
+            if k in QUANT_IN_ROUND:
+                a_quant(QUANT_IN_ROUND[k])
+                if k == 2:
+                    mm(4)
+            if 0 <= kd:
+                p4(kd, 0)
+                if last:
+                    st0(kd, 0, 512)
+                    p5(kd, 0, 512, False)
+            if kn < 8:
+                nm(kn)
+                p2(kn)
+            if k < 8:
+                rec(k)
+            if kn < 8:
+                sq(kn)
+                dd(kn)
+            for s in COPY_IN_ROUND.get(k, ()):
+                a_copy(s)
+            if 0 <= kd:
+                p4(kd, 1)
+                if last:
+                    st0(kd, 512, C)
+                    p5(kd, 512, C, True)
+                    st1(kd - 1, 0, C)
+                    st1(kd, 0, 512)
+                    st1(kd, 512, C)
                 else:
-                    st_out(kd, 0, C, False)
-            if k == 2:
-                a_quant(2)
-            if k == 4:
-                a_quant(3)
-            if kr < 8:
-                st_c(kr)
-                st_xc(kr, kr >= 6)
-            if k >= 2 and k + 2 < 8:
-                mm(k + 2)
+                    st0(kd, 0, C)
+                    p5(kd, 0, C, False)
+                    if kd >= 1:
+                        st1(kd - 1, 0, C)
+            if 2 <= k and k + 3 < 8:
+                mm(k + 3)
+            if k < 8:
+                cc(k)
+                p3(k)
             if ka < 8:
-                st_a(ka, 0)
-                st_a(ka, 1)
-                st_nm(ka)
-                st_b(ka)
-            if k == 1:
-                a_copy(3, 0, 0)
-            if k == 2:
-                a_copy(3, 1, 0)
+                p1(ka, 0)
+                p1(ka, 1)

@@ -347,8 +347,14 @@ def tile_swintransformerblock_pb_kernel(tc, o_attn, out_w, out_b, ada1_scale, ad
                 p2(kn)
             if k < 8:
                 rec(k)
+            woven = 0 <= kd and kn < 8
+            if woven:
+                p5(kd, 0, 256, False)
             if kn < 8:
                 sq(kn)
+            if woven:
+                p5(kd, 256, 512, False)
+            if kn < 8:
                 dd(kn)
             for s in COPY_IN_ROUND.get(k, ()):
                 a_copy(s)
@@ -362,7 +368,7 @@ def tile_swintransformerblock_pb_kernel(tc, o_attn, out_w, out_b, ada1_scale, ad
                     st1(kd, 512, C)
                 else:
                     st0(kd, 0, C)
-                    p5(kd, 0, C, False)
+                    p5(kd, 512 if woven else 0, C, False)
                     if kd >= 1:
                         st1(kd - 1, 0, C)
             if 2 <= k and k + 3 < 8:

@@ -256,15 +256,15 @@ def tile_swintransformerblock_pb_kernel(tc, o_attn, out_w, out_b, ada1_scale, ad
 
         def p3(k):
             a = order[k]
-            xc = work.tile([P, C], F32, name="xc", bufs=2)
+            xc = work.tile([P, C], F32, name="xc", bufs=3)
             xcs[k] = xc
             nc.gpsimd.tensor_scalar(out=xc[:], in0=x_raw[a][:], scalar1=1.0, scalar2=sts[k][:, 8:9], op0=ALU.mult, op1=ALU.add)
 
-        def p4(k, h):
-            if h == 0:
+        def p4(k, lo, hi):
+            if lo == 0:
                 ys[k] = work.tile([P, C], F32, name="y")
                 ybs[k] = work.tile([P, C], FP8, name="yb", bufs=4)
-            cols = slice(512 * h, 512 * (h + 1))
+            cols = slice(lo, hi)
             nc.vector.scalar_tensor_tensor(out=ys[k][:, cols], in0=ts[k][:, cols], scalar=sts[k][:, 7:8], in1=xcs[k][:, cols], op0=ALU.mult, op1=ALU.add)
 
         def st0(k, lo, hi):
@@ -338,7 +338,7 @@ def tile_swintransformerblock_pb_kernel(tc, o_attn, out_w, out_b, ada1_scale, ad
                 if k == 2:
                     mm(4)
             if 0 <= kd:
-                p4(kd, 0)
+                p4(kd, 0, 512)
                 if last:
                     st0(kd, 0, 512)
                     p5(kd, 0, 512, False)
@@ -359,7 +359,11 @@ def tile_swintransformerblock_pb_kernel(tc, o_attn, out_w, out_b, ada1_scale, ad
             for s in COPY_IN_ROUND.get(k, ()):
                 a_copy(s)
             if 0 <= kd:
-                p4(kd, 1)
+                p4(kd, 512, 768)
+                if k < 8:
+                    cc(k)
+                    p3(k)
+                p4(kd, 768, C)
                 if last:
                     st0(kd, 512, C)
                     p5(kd, 512, C, True)
@@ -373,7 +377,7 @@ def tile_swintransformerblock_pb_kernel(tc, o_attn, out_w, out_b, ada1_scale, ad
                         st1(kd - 1, 0, C)
             if 2 <= k and k + 3 < 8:
                 mm(k + 3)
-            if k < 8:
+            if kd < 0:
                 cc(k)
                 p3(k)
             if ka < 8:

@@ -254,10 +254,13 @@ def tile_swintransformerblock_pb_kernel(tc, o_attn, out_w, out_b, ada1_scale, ad
             a = order[k]
             nc.vector.tensor_scalar(out=st[:, 8:9], in0=st[:, 2:3], scalar1=st[:, 7:8], scalar2=ada_f[:, 8 + a:9 + a], op0=ALU.mult, op1=ALU.add)
 
-        def p3(k):
+        def p3(k, on_vector):
             a = order[k]
             xc = work.tile([P, C], F32, name="xc", bufs=3)
             xcs[k] = xc
+            if on_vector:
+                nc.vector.tensor_scalar(out=xc[:], in0=x_raw[a][:], scalar1=sts[k][:, 8:9], scalar2=None, op0=ALU.add)
+                return
             nc.gpsimd.tensor_scalar(out=xc[:], in0=x_raw[a][:], scalar1=1.0, scalar2=sts[k][:, 8:9], op0=ALU.mult, op1=ALU.add)
 
         def p4(k, lo, hi):
@@ -328,58 +331,74 @@ def tile_swintransformerblock_pb_kernel(tc, o_attn, out_w, out_b, ada1_scale, ad
         a_turn(6)
         a_turn(7)
 
-        for k in range(10):
+        for k in range(6):
             kn = k + 1
             kd = k - 2
             ka = k + 2
-            last = kd == 7
             if k in QUANT_IN_ROUND:
                 a_quant(QUANT_IN_ROUND[k])
                 if k == 2:
                     mm(4)
             if 0 <= kd:
                 p4(kd, 0, 512)
-                if last:
-                    st0(kd, 0, 512)
-                    p5(kd, 0, 512, False)
-            if kn < 8:
-                nm(kn)
-                p2(kn)
-            if k < 8:
-                rec(k)
-            woven = 0 <= kd and kn < 8
-            if woven:
+            nm(kn)
+            p2(kn)
+            rec(k)
+            if 0 <= kd:
                 p5(kd, 0, 256, False)
-            if kn < 8:
-                sq(kn)
-            if woven:
+            sq(kn)
+            if 0 <= kd:
                 p5(kd, 256, 512, False)
-            if kn < 8:
-                dd(kn)
+            dd(kn)
             for s in COPY_IN_ROUND.get(k, ()):
                 a_copy(s)
             if 0 <= kd:
                 p4(kd, 512, 768)
-                if k < 8:
-                    cc(k)
-                    p3(k)
+            cc(k)
+            p3(k, False)
+            if 0 <= kd:
                 p4(kd, 768, C)
-                if last:
-                    st0(kd, 512, C)
-                    p5(kd, 512, C, True)
+                st0(kd, 0, C)
+                p5(kd, 512, C, False)
+                if kd >= 1:
                     st1(kd - 1, 0, C)
-                    st1(kd, 0, 512)
-                    st1(kd, 512, C)
-                else:
-                    st0(kd, 0, C)
-                    p5(kd, 512 if woven else 0, C, False)
-                    if kd >= 1:
-                        st1(kd - 1, 0, C)
             if 2 <= k and k + 3 < 8:
                 mm(k + 3)
-            if kd < 0:
-                cc(k)
-                p3(k)
-            if ka < 8:
-                p1(ka, 0)
-                p1(ka, 1)
+            p1(ka, 0)
+            p1(ka, 1)
+
+        def y_part(k, lo, hi, cast_on_vector):
+            p4(k, lo, hi)
+            st0(k, lo, hi)
+            p5(k, lo, hi, cast_on_vector)
+
+        p4(4, 0, 512)
+        st0(4, 0, 512)
+        nm(7)
+        p2(7)
+        rec(6)
+        p5(4, 0, 256, False)
+        sq(7)
+        p5(4, 256, 512, False)
+        dd(7)
+        p4(4, 512, 768)
+        cc(6)
+        p4(4, 768, C)
+        st0(4, 512, C)
+        p5(4, 512, C, False)
+        st1(3, 0, C)
+        p3(6, True)
+        y_part(5, 0, 512, False)
+        y_part(5, 512, C, False)
+        st1(4, 0, C)
+        rec(7)
+        y_part(6, 0, 512, False)
+        cc(7)
+        y_part(6, 512, C, False)
+        st1(5, 0, C)
+        p3(7, True)
+        y_part(7, 0, 512, False)
+        st1(6, 0, C)
+        y_part(7, 512, C, True)
+        st1(7, 0, 512)
+        st1(7, 512, C)

@@ -340,10 +340,12 @@ def tile_swintransformerblock_pb_kernel(tc, o_attn, out_w, out_b, ada1_scale, ad
                 if k == 2:
                     mm(4)
             if 0 <= kd:
-                p4(kd, 0, 512)
+                p4(kd, 0, 256)
             nm(kn)
             p2(kn)
             rec(k)
+            if 0 <= kd:
+                p4(kd, 256, 512)
             if 0 <= kd:
                 p5(kd, 0, 256, False)
             sq(kn)
@@ -352,12 +354,10 @@ def tile_swintransformerblock_pb_kernel(tc, o_attn, out_w, out_b, ada1_scale, ad
             dd(kn)
             for s in COPY_IN_ROUND.get(k, ()):
                 a_copy(s)
-            if 0 <= kd:
-                p4(kd, 512, 768)
             cc(k)
             p3(k, False)
             if 0 <= kd:
-                p4(kd, 768, C)
+                p4(kd, 512, C)
                 st0(kd, 0, C)
                 p5(kd, 512, C, False)
                 if kd >= 1:

@@ -42,21 +42,15 @@ def tile_swintransformerblock_pb_kernel(tc, o_attn, out_w, out_b, ada1_scale, ad
 
         ctx.enter_context(tc.manual_schedule())
 
-        misc = const.tile([P, C + P], BF16, name="misc")
-        nc.vector.memset(misc[:], 0.0)
-        nc.scalar.dma_start(out=misc[0:1, 0:C], in_=out_b.rearrange("(o n) -> o n", o=1))
-        nc.scalar.dma_start(out=misc[0:8, C:C + P], in_=ada1_scale.rearrange("o (a p) i -> (o a) (p i)", p=P))
-        nc.scalar.dma_start(out=misc[8:16, C:C + P], in_=ada1_shift.rearrange("o (a p) i -> (o a) (p i)", p=P))
-        ones_b = const.tile([P, P], BF16, name="ones_b")
-        nc.vector.memset(ones_b[:], 1.0)
-        zeros_b = const.tile([P, 512], BF16, name="zeros_b")
-        nc.vector.memset(zeros_b[:], 0.0)
-        pd = ps_t.tile([P, 512], F32, name="pd", tag="tp")
-        for i in range(4):
-            nc.tensor.matmul(pd[:], lhsT=ones_b[:], rhs=zeros_b[:], start=True, stop=True)
+        ada_in = const.tile([P, P], BF16, name="ada_in")
+        nc.vector.memset(ada_in[:], 0.0)
+        nc.scalar.dma_start(out=ada_in[0:8, :], in_=ada1_scale.rearrange("o (a p) i -> (o a) (p i)", p=P))
+        nc.scalar.dma_start(out=ada_in[8:16, :], in_=ada1_shift.rearrange("o (a p) i -> (o a) (p i)", p=P))
         warm = const.tile([P, 2], F32, name="warm")
         nc.vector.memset(warm[:, 0:1], 1.0)
         nc.scalar.activation(out=warm[:, 1:2], in_=warm[:, 0:1], func=ACT.Sqrt)
+        ones_b = const.tile([P, P], BF16, name="ones_b")
+        nc.vector.memset(ones_b[:], 1.0)
 
         a_raw = []
         w_raw = []
@@ -89,6 +83,9 @@ def tile_swintransformerblock_pb_kernel(tc, o_attn, out_w, out_b, ada1_scale, ad
         ident_b = const.tile([P, P], BF16, name="ident_b")
         nc.vector.tensor_copy(out=ident_b[:], in_=ident_f[:])
 
+        bias_in = const.tile([P, C], BF16, name="bias_in")
+        nc.vector.memset(bias_in[:], 0.0)
+        nc.scalar.dma_start(out=bias_in[0:1, :], in_=out_b.rearrange("(o n) -> o n", o=1))
         bias_bc = const.tile([P, C], BF16, name="bias_bc")
         ada_f = const.tile([P, 16], F32, name="ada_f")
         ig = const.tile([P, 16], F32, name="ig")
@@ -96,7 +93,7 @@ def tile_swintransformerblock_pb_kernel(tc, o_attn, out_w, out_b, ada1_scale, ad
         def bias_mm():
             pb = ps_a.tile([P, C], BF16, name="pb", tag="acc")
             for h in range(2):
-                nc.tensor.matmul(pb[:, 512 * h:512 * (h + 1)], lhsT=ones_b[:], rhs=misc[:, 512 * h:512 * (h + 1)], start=True, stop=True)
+                nc.tensor.matmul(pb[:, 512 * h:512 * (h + 1)], lhsT=ones_b[:], rhs=bias_in[:, 512 * h:512 * (h + 1)], start=True, stop=True)
             return pb
 
         def bias_copy(pb):
@@ -105,7 +102,7 @@ def tile_swintransformerblock_pb_kernel(tc, o_attn, out_w, out_b, ada1_scale, ad
 
         def ada_prep():
             pa = ps_t.tile([P, P], BF16, name="pa", tag="tp")
-            nc.tensor.transpose(pa[:], misc[:, C:C + P], ident_b[:])
+            nc.tensor.transpose(pa[:], ada_in[:], ident_b[:])
             nc.scalar.copy(out=ada_f[:], in_=pa[:, 0:16])
 
         def ig_prep():

@@ -44,13 +44,13 @@ def tile_swintransformerblock_pb_kernel(tc, o_attn, out_w, out_b, ada1_scale, ad
 
         ada_in = const.tile([P, P], BF16, name="ada_in")
         nc.vector.memset(ada_in[:], 0.0)
-        nc.scalar.dma_start(out=ada_in[0:8, :], in_=ada1_scale.rearrange("o (a p) i -> (o a) (p i)", p=P))
-        nc.scalar.dma_start(out=ada_in[8:16, :], in_=ada1_shift.rearrange("o (a p) i -> (o a) (p i)", p=P))
         warm = const.tile([P, 2], F32, name="warm")
         nc.vector.memset(warm[:, 0:1], 1.0)
         nc.scalar.activation(out=warm[:, 1:2], in_=warm[:, 0:1], func=ACT.Sqrt)
         ones_b = const.tile([P, P], BF16, name="ones_b")
         nc.vector.memset(ones_b[:], 1.0)
+        bias_in = const.tile([P, C], BF16, name="bias_in")
+        nc.vector.memset(bias_in[:], 0.0)
 
         a_raw = []
         w_raw = []
@@ -66,6 +66,9 @@ def tile_swintransformerblock_pb_kernel(tc, o_attn, out_w, out_b, ada1_scale, ad
             load_a(s)
         for j in range(8):
             nc.sync.dma_start(out=w_raw[j][:], in_=out_w[P * j:P * (j + 1), :])
+        nc.sync.dma_start(out=bias_in[0:1, :], in_=out_b.rearrange("(o n) -> o n", o=1))
+        nc.sync.dma_start(out=ada_in[0:8, :], in_=ada1_scale.rearrange("o (a p) i -> (o a) (p i)", p=P))
+        nc.sync.dma_start(out=ada_in[8:16, :], in_=ada1_shift.rearrange("o (a p) i -> (o a) (p i)", p=P))
         for s in range(2, 8):
             load_a(s)
         order = [1, 2, 3, 4, 5, 6, 7, 0]
@@ -83,9 +86,6 @@ def tile_swintransformerblock_pb_kernel(tc, o_attn, out_w, out_b, ada1_scale, ad
         ident_b = const.tile([P, P], BF16, name="ident_b")
         nc.vector.tensor_copy(out=ident_b[:], in_=ident_f[:])
 
-        bias_in = const.tile([P, C], BF16, name="bias_in")
-        nc.vector.memset(bias_in[:], 0.0)
-        nc.scalar.dma_start(out=bias_in[0:1, :], in_=out_b.rearrange("(o n) -> o n", o=1))
         bias_bc = const.tile([P, C], BF16, name="bias_bc")
         ada_f = const.tile([P, 16], F32, name="ada_f")
         ig = const.tile([P, 16], F32, name="ig")
@@ -285,7 +285,6 @@ def tile_swintransformerblock_pb_kernel(tc, o_attn, out_w, out_b, ada1_scale, ad
         a_copy(0)
         a_turn(1)
         a_copy(1)
-        ada_prep()
         for j in range(8):
             sort_words("w%d" % j)
             w_turn_copy(j)
@@ -303,6 +302,7 @@ def tile_swintransformerblock_pb_kernel(tc, o_attn, out_w, out_b, ada1_scale, ad
         w_quant(7, 1)
         mmh(0, 0)
         bias_copy(pb)
+        ada_prep()
         a_turn(2)
         a_copy(2)
         mmh(0, 1)

@@ -19,7 +19,7 @@ C = 1024
 EPS = 1e-5
 Y_SCALE = 150.0
 
-SORTED = ("w0", "w1", "w2", "w3", "w4", "w5", "w6", "a2", "a3")
+SORTED = ("w1", "w3", "w5", "a2", "a3")
 COPY_IN_ROUND = {0: (5,), 1: (6, 7)}
 QUANT_IN_ROUND = {2: 2, 3: 3}
 
@@ -105,9 +105,11 @@ def tile_swintransformerblock_pb_kernel(tc, o_attn, out_w, out_b, ada1_scale, ad
             nc.tensor.transpose(pa[:], ada_in[:], ident_b[:])
             nc.scalar.copy(out=ada_f[:], in_=pa[:, 0:16])
 
-        def ig_prep():
-            nc.vector.reciprocal(out=ig[:, 0:8], in_=ada_f[:, 0:8])
-            nc.vector.tensor_scalar(out=ig[:, 8:16], in0=ig[:, 0:8], scalar1=EPS, scalar2=None, op0=ALU.mult)
+        def ig_prep(step):
+            if step == 0:
+                nc.vector.reciprocal(out=ig[:, 0:8], in_=ada_f[:, 0:8])
+            else:
+                nc.vector.tensor_scalar(out=ig[:, 8:16], in0=ig[:, 0:8], scalar1=EPS, scalar2=None, op0=ALU.mult)
 
         sorted_words = {}
 
@@ -177,6 +179,16 @@ def tile_swintransformerblock_pb_kernel(tc, o_attn, out_w, out_b, ada1_scale, ad
                 out=gw[:, :, P * jj:P * (jj + 1), :],
                 in_=pt[:].rearrange("p (g u n) -> p g n u", g=2, u=2, n=P),
             )
+
+        def w_turn_copy_last(j):
+            h, jj = divmod(j, 4)
+            gw = w_grp[h][:].bitcast(F32).rearrange("p (g n u) -> p g n u", g=2, n=512, u=2)
+            for g in range(2):
+                pt = ps_t.tile([P, 256], F32, name="pt", tag="tp")
+                for u in range(2):
+                    nc.tensor.transpose(pt[:, u * P:(u + 1) * P], turn_src("w%d" % j, w_raw[j], g, u), ident_f[:])
+                copy = nc.scalar.copy if g == 0 else nc.vector.tensor_copy
+                copy(out=gw[:, g, P * jj:P * (jj + 1), :], in_=pt[:].rearrange("p (u n) -> p n u", u=2, n=P))
 
         def w_quant(j0, n):
             h, jj = divmod(j0, 4)
@@ -256,7 +268,9 @@ def tile_swintransformerblock_pb_kernel(tc, o_attn, out_w, out_b, ada1_scale, ad
             xc = work.tile([P, C], F32, name="xc", bufs=3)
             xcs[k] = xc
             if on_vector:
-                nc.vector.tensor_scalar(out=xc[:], in0=x_raw[a][:], scalar1=sts[k][:, 8:9], scalar2=None, op0=ALU.add)
+                for h in range(2):
+                    cols = slice(512 * h, 512 * (h + 1))
+                    nc.vector.tensor_scalar(out=xc[:, cols], in0=x_raw[a][:, cols], scalar1=sts[k][:, 8:9], scalar2=None, op0=ALU.add)
                 return
             nc.gpsimd.tensor_scalar(out=xc[:], in0=x_raw[a][:], scalar1=1.0, scalar2=sts[k][:, 8:9], op0=ALU.mult, op1=ALU.add)
 
@@ -287,7 +301,8 @@ def tile_swintransformerblock_pb_kernel(tc, o_attn, out_w, out_b, ada1_scale, ad
         a_copy(1)
         for j in range(8):
             sort_words("w%d" % j)
-            w_turn_copy(j)
+            if j < 7:
+                w_turn_copy(j)
             if j == 3:
                 a_quant(0)
             if j == 5:
@@ -297,8 +312,9 @@ def tile_swintransformerblock_pb_kernel(tc, o_attn, out_w, out_b, ada1_scale, ad
         sort_words("a2")
         sort_words("a3")
         w_quant(4, 2)
-        pb = bias_mm()
         w_quant(6, 1)
+        w_turn_copy_last(7)
+        pb = bias_mm()
         w_quant(7, 1)
         mmh(0, 0)
         bias_copy(pb)
@@ -312,10 +328,11 @@ def tile_swintransformerblock_pb_kernel(tc, o_attn, out_w, out_b, ada1_scale, ad
         mmh(1, 1)
         p1(0, 0)
         p1(0, 1)
+        ig_prep(0)
         nm(0)
         p2(0)
-        ig_prep()
         p1(1, 0)
+        ig_prep(1)
         a_quant(1)
         a_turn(4)
         sq(0)
@@ -338,9 +355,12 @@ def tile_swintransformerblock_pb_kernel(tc, o_attn, out_w, out_b, ada1_scale, ad
                     mm(4)
             if 0 <= kd:
                 p4(kd, 0, 256)
+            if k == 0:
+                rec(k)
             nm(kn)
             p2(kn)
-            rec(k)
+            if k > 0:
+                rec(k)
             if 0 <= kd:
                 p4(kd, 256, 512)
             if 0 <= kd:

from contextlib import ExitStack

import concourse.mybir as mybir
from concourse.masks import make_identity

FLOPS = 2 * 1024 * 1024 * 1024

F32 = mybir.dt.float32
BF16 = mybir.dt.bfloat16
U32 = mybir.dt.uint32
U8 = mybir.dt.uint8
FP8X4 = mybir.dt.float8_e4m3fn_x4
FP8 = mybir.dt.float8_e4m3fn
ALU = mybir.AluOpType
ACT = mybir.ActivationFunctionType

P = 128
C = 1024
EPS = 1e-5
Y_SCALE = 150.0

SORTED = ("w1", "w3", "w5", "a2", "a3")
COPY_IN_ROUND = {0: (5,), 1: (6, 7)}
QUANT_IN_ROUND = {2: 2, 3: 3}


def tile_swintransformerblock_pb_kernel(tc, o_attn, out_w, out_b, ada1_scale, ada1_shift, x, out_0, out_1):
    nc = tc.nc
    o_flat = o_attn.flatten_outer_dims()
    x_flat = x.flatten_outer_dims()
    y_flat = out_0.flatten_outer_dims()
    yb_flat = out_1.flatten_outer_dims()

    with ExitStack() as ctx:
        const = ctx.enter_context(tc.tile_pool(name="const", bufs=1))
        raw = ctx.enter_context(tc.tile_pool(name="raw", bufs=1))
        agrp = ctx.enter_context(tc.tile_pool(name="agrp", bufs=4))
        work = ctx.enter_context(tc.tile_pool(name="work", bufs=3))
        stat = ctx.enter_context(tc.tile_pool(name="stat", bufs=8))
        ps_t = ctx.enter_context(tc.psum_pool(name="ps_t", bufs=4))
        ps_a = ctx.enter_context(tc.psum_pool(name="ps_a", bufs=4))

        ctx.enter_context(tc.manual_schedule())

        ada_in = const.tile([P, P], BF16, name="ada_in")
        nc.vector.memset(ada_in[:], 0.0)
        warm = const.tile([P, 2], F32, name="warm")
        nc.vector.memset(warm[:, 0:1], 1.0)
        nc.scalar.activation(out=warm[:, 1:2], in_=warm[:, 0:1], func=ACT.Sqrt)
        ones_b = const.tile([P, P], BF16, name="ones_b")
        nc.vector.memset(ones_b[:], 1.0)
        bias_in = const.tile([P, C], BF16, name="bias_in")
        nc.vector.memset(bias_in[:], 0.0)

        a_raw = []
        w_raw = []
        x_raw = {}
        for s in range(8):
            a_raw.append(raw.tile([P, C], BF16, name="a_raw%d" % s))
            w_raw.append(raw.tile([P, C], BF16, name="w_raw%d" % s))

        def load_a(s):
            nc.sync.dma_start(out=a_raw[s][:], in_=o_flat[P * s:P * (s + 1), :])

        for s in range(2):
            load_a(s)
        for j in range(8):
            nc.sync.dma_start(out=w_raw[j][:], in_=out_w[P * j:P * (j + 1), :])
        nc.sync.dma_start(out=bias_in[0:1, :], in_=out_b.rearrange("(o n) -> o n", o=1))
        nc.sync.dma_start(out=ada_in[0:8, :], in_=ada1_scale.rearrange("o (a p) i -> (o a) (p i)", p=P))
        nc.sync.dma_start(out=ada_in[8:16, :], in_=ada1_shift.rearrange("o (a p) i -> (o a) (p i)", p=P))
        for s in range(2, 8):
            load_a(s)
        order = [1, 2, 3, 4, 5, 6, 7, 0]
        for a in order:
            x_raw[a] = raw.tile([P, C], BF16, name="x_raw%d" % a)
            nc.sync.dma_start(out=x_raw[a][:], in_=x_flat[P * a:P * (a + 1), :])

        ident_f = const.tile([P, P], F32, name="ident_f")
        make_identity(nc, ident_f[:])
        perm_f = const.tile([P, P], F32, name="perm_f")
        nc.vector.tensor_copy(
            out=perm_f[:].rearrange("p (r w c) -> p w r c", r=8, w=2, c=8),
            in_=ident_f[:].rearrange("p (w r c) -> p w r c", w=2, r=8, c=8),
        )
        ident_b = const.tile([P, P], BF16, name="ident_b")
        nc.vector.tensor_copy(out=ident_b[:], in_=ident_f[:])

        bias_bc = const.tile([P, C], BF16, name="bias_bc")
        ada_f = const.tile([P, 16], F32, name="ada_f")
        ig = const.tile([P, 16], F32, name="ig")

        def bias_mm():
            pb = ps_a.tile([P, C], BF16, name="pb", tag="acc")
            for h in range(2):
                nc.tensor.matmul(pb[:, 512 * h:512 * (h + 1)], lhsT=ones_b[:], rhs=bias_in[:, 512 * h:512 * (h + 1)], start=True, stop=True)
            return pb

        def bias_copy(pb):
            for h in range(2):
                nc.scalar.copy(out=bias_bc[:, 512 * h:512 * (h + 1)], in_=pb[:, 512 * h:512 * (h + 1)])

        def ada_prep():
            pa = ps_t.tile([P, P], BF16, name="pa", tag="tp")
            nc.tensor.transpose(pa[:], ada_in[:], ident_b[:])
            nc.scalar.copy(out=ada_f[:], in_=pa[:, 0:16])

        def ig_prep(step):
            if step == 0:
                nc.vector.reciprocal(out=ig[:, 0:8], in_=ada_f[:, 0:8])
            else:
                nc.vector.tensor_scalar(out=ig[:, 8:16], in0=ig[:, 0:8], scalar1=EPS, scalar2=None, op0=ALU.mult)

        sorted_words = {}

        def sort_words(key):
            if key not in SORTED:
                return
            src = a_raw[int(key[1])] if key[0] == "a" else w_raw[int(key[1])]
            dst = raw.tile([P, 512], F32, name="sw_%s" % key)
            nc.vector.tensor_copy(
                out=dst[:].rearrange("p (g u q) -> p g u q", g=2, u=2, q=P),
                in_=src[:].bitcast(F32).rearrange("p (g q u) -> p g u q", g=2, q=P, u=2),
            )
            sorted_words[key] = dst

        def turn_src(key, src, g, u):
            if key in sorted_words:
                lo = 256 * g + P * u
                return sorted_words[key][:, lo:lo + P]
            return src[:].bitcast(F32)[:, 256 * g + u:256 * (g + 1):2]

        a_state = {}
        a_bank = {}

        def a_turn(s):
            pt = ps_t.tile([P, 512], F32, name="pt", tag="tp")
            a_bank[s] = pt
            for u in range(2):
                for g in range(2):
                    nc.tensor.transpose(pt[:, (2 * u + g) * P:(2 * u + g + 1) * P], turn_src("a%d" % s, a_raw[s], g, u), perm_f[:])

        def a_copy(s):
            wi, s2 = divmod(s, 2)
            if s2 == 0:
                a_state[wi] = agrp.tile([P, 2048], BF16, name="a_grp", align_bytes=64)
            gw = a_state[wi][:].bitcast(F32).rearrange("p (q j u) -> p q j u", q=16, j=32, u=2)
            pv = a_bank[s][:].rearrange("p (u q jj) -> p q jj u", u=2, q=16, jj=16)
            if s2 == 0:
                nc.scalar.copy(out=gw[:, :, 4:20, :], in_=pv)
            else:
                nc.scalar.copy(out=gw[:, :, 20:32, :], in_=pv[:, :, 0:12, :])
                nc.scalar.copy(out=gw[:, :, 0:4, :], in_=pv[:, :, 12:16, :])

        a_cs = {}

        def a_quant(wi):
            codes = agrp.tile([P, 512], U32, name="a_codes", align_bytes=64)
            scales = agrp.tile([P, 512], U8, name="a_scales", align_bytes=64)
            nc.vector.quantize_mx(out=codes[:].bitcast(FP8X4), scales=scales[:], in_=a_state[wi][:])
            a_cs[wi] = (codes, scales)

        w_grp = []
        w_codes = []
        w_scales = []
        for h in range(2):
            w_grp.append(const.tile([P, 4096], BF16, name="w_grp%d" % h, align_bytes=64))
            w_codes.append(const.tile([P, 1024], U32, name="w_codes%d" % h, align_bytes=64))
            w_scales.append(const.tile([P, 1024], U8, name="w_scales%d" % h, align_bytes=64))

        def w_turn_copy(j):
            h, jj = divmod(j, 4)
            pt = ps_t.tile([P, 512], F32, name="pt", tag="tp")
            for g in range(2):
                for u in range(2):
                    nc.tensor.transpose(pt[:, (2 * g + u) * P:(2 * g + u + 1) * P], turn_src("w%d" % j, w_raw[j], g, u), ident_f[:])
            gw = w_grp[h][:].bitcast(F32).rearrange("p (g n u) -> p g n u", g=2, n=512, u=2)
            nc.scalar.copy(
                out=gw[:, :, P * jj:P * (jj + 1), :],
                in_=pt[:].rearrange("p (g u n) -> p g n u", g=2, u=2, n=P),
            )

        def w_turn_copy_last(j):
            h, jj = divmod(j, 4)
            gw = w_grp[h][:].bitcast(F32).rearrange("p (g n u) -> p g n u", g=2, n=512, u=2)
            for g in range(2):
                pt = ps_t.tile([P, 256], F32, name="pt", tag="tp")
                for u in range(2):
                    nc.tensor.transpose(pt[:, u * P:(u + 1) * P], turn_src("w%d" % j, w_raw[j], g, u), ident_f[:])
                copy = nc.scalar.copy if g == 0 else nc.vector.tensor_copy
                copy(out=gw[:, g, P * jj:P * (jj + 1), :], in_=pt[:].rearrange("p (u n) -> p n u", u=2, n=P))

        def w_quant(j0, n):
            h, jj = divmod(j0, 4)
            for g in range(2):
                lo = 512 * g + P * jj
                nc.vector.quantize_mx(
                    out=w_codes[h][:, lo:lo + P * n].bitcast(FP8X4),
                    scales=w_scales[h][:, lo:lo + P * n],
                    in_=w_grp[h][:, 4 * lo:4 * (lo + P * n)],
                )

        accs = {}
        sts = {}
        ts = {}
        xcs = {}
        ys = {}
        ybs = {}

        def mmh(k, h):
            codes, scales = a_cs[k // 2]
            acc = ps_a.tile([P, 512], F32, name="acc")
            accs[(k, h)] = acc
            for g in range(2):
                lo = 256 * g + P * (k % 2)
                nc.tensor.matmul_mx(
                    out=acc[:],
                    lhsT=codes[:, lo:lo + P].bitcast(FP8X4),
                    lhsT_scale=scales[:, lo:lo + P],
                    rhs=w_codes[h][:, 512 * g:512 * (g + 1)].bitcast(FP8X4),
                    rhs_scale=w_scales[h][:, 512 * g:512 * (g + 1)],
                    start=(g == 0),
                    stop=(g == 1),
                )

        def mm(k):
            mmh(k, 0)
            mmh(k, 1)

        def p1(k, h):
            if h == 0:
                sts[k] = stat.tile([P, 16], F32, name="st")
                ts[k] = work.tile([P, C], F32, name="t", bufs=6)
            cols = slice(512 * h, 512 * (h + 1))
            nc.vector.scalar_tensor_tensor(
                out=ts[k][:, cols], in0=accs[(k, h)][:], scalar=1.0, in1=bias_bc[:, cols],
                op0=ALU.mult, op1=ALU.add, accum_out=sts[k][:, h:h + 1],
            )

        def nm(k):
            st = sts[k]
            nc.vector.tensor_scalar(out=st[:, 2:3], in0=st[:, 0:1], scalar1=st[:, 1:2], scalar2=-1.0 / C, op0=ALU.add, op1=ALU.mult)

        def p2(k):
            st = sts[k]
            junk = work.tile([P, C], F32, name="junk", bufs=2)
            nc.scalar.activation(out=junk[:], in_=ts[k][:], func=ACT.Square, bias=st[:, 2:3], scale=1.0, accum_out=st[:, 3:4])

        def sq(k):
            st = sts[k]
            nc.scalar.activation(out=st[:, 4:5], in_=st[:, 3:4], func=ACT.Sqrt, scale=1.0 / (C - 1))

        def dd(k):
            st = sts[k]
            a = order[k]
            nc.scalar.activation(out=st[:, 5:6], in_=st[:, 4:5], func=ACT.Identity, scale=ig[:, a:a + 1], bias=ig[:, 8 + a:9 + a])

        def rec(k):
            nc.vector.reciprocal(out=sts[k][:, 7:8], in_=sts[k][:, 5:6])

        def cc(k):
            st = sts[k]
            a = order[k]
            nc.vector.tensor_scalar(out=st[:, 8:9], in0=st[:, 2:3], scalar1=st[:, 7:8], scalar2=ada_f[:, 8 + a:9 + a], op0=ALU.mult, op1=ALU.add)

        def p3(k, on_vector):
            a = order[k]
            xc = work.tile([P, C], F32, name="xc", bufs=3)
            xcs[k] = xc
            if on_vector:
                for h in range(2):
                    cols = slice(512 * h, 512 * (h + 1))
                    nc.vector.tensor_scalar(out=xc[:, cols], in0=x_raw[a][:, cols], scalar1=sts[k][:, 8:9], scalar2=None, op0=ALU.add)
                return
            nc.gpsimd.tensor_scalar(out=xc[:], in0=x_raw[a][:], scalar1=1.0, scalar2=sts[k][:, 8:9], op0=ALU.mult, op1=ALU.add)

        def p4(k, lo, hi):
            if lo == 0:
                ys[k] = work.tile([P, C], F32, name="y")
                ybs[k] = work.tile([P, C], FP8, name="yb", bufs=4)
            cols = slice(lo, hi)
            nc.vector.scalar_tensor_tensor(out=ys[k][:, cols], in0=ts[k][:, cols], scalar=sts[k][:, 7:8], in1=xcs[k][:, cols], op0=ALU.mult, op1=ALU.add)

        def st0(k, lo, hi):
            a = order[k]
            nc.sync.dma_start(out=y_flat[P * a:P * (a + 1), lo:hi], in_=ys[k][:, lo:hi])

        def p5(k, lo, hi, on_vector):
            if on_vector:
                nc.vector.tensor_scalar(out=ybs[k][:, lo:hi], in0=ys[k][:, lo:hi], scalar1=Y_SCALE, scalar2=None, op0=ALU.mult, saturate=False)
            else:
                nc.scalar.activation(out=ybs[k][:, lo:hi], in_=ys[k][:, lo:hi], func=ACT.Copy, scale=Y_SCALE, saturate=False)

        def st1(k, lo, hi):
            a = order[k]
            nc.sync.dma_start(out=yb_flat[P * a:P * (a + 1), lo:hi], in_=ybs[k][:, lo:hi].bitcast(U8))

        a_turn(0)
        a_copy(0)
        a_turn(1)
        a_copy(1)
        for j in range(8):
            sort_words("w%d" % j)
            if j < 7:
                w_turn_copy(j)
            if j == 3:
                a_quant(0)
            if j == 5:
                w_quant(0, 2)
            if j == 6:
                w_quant(2, 2)
        sort_words("a2")
        sort_words("a3")
        w_quant(4, 2)
        w_quant(6, 1)
        w_turn_copy_last(7)
        pb = bias_mm()
        w_quant(7, 1)
        mmh(0, 0)
        bias_copy(pb)
        ada_prep()
        a_turn(2)
        a_copy(2)
        mmh(0, 1)
        a_turn(3)
        a_copy(3)
        mmh(1, 0)
        mmh(1, 1)
        p1(0, 0)
        p1(0, 1)
        ig_prep(0)
        nm(0)
        p2(0)
        p1(1, 0)
        ig_prep(1)
        a_quant(1)
        a_turn(4)
        sq(0)
        dd(0)
        a_copy(4)
        p1(1, 1)
        mm(2)
        a_turn(5)
        mm(3)
        a_turn(6)
        a_turn(7)

        for k in range(6):
            kn = k + 1
            kd = k - 2
            ka = k + 2
            if k in QUANT_IN_ROUND:
                a_quant(QUANT_IN_ROUND[k])
                if k == 2:
                    mm(4)
            if 0 <= kd:
                p4(kd, 0, 256)
            if k == 0:
                rec(k)
            nm(kn)
            p2(kn)
            if k > 0:
                rec(k)
            if 0 <= kd:
                p4(kd, 256, 512)
            if 0 <= kd:
                p5(kd, 0, 256, False)
            sq(kn)
            if 0 <= kd:
                p5(kd, 256, 512, False)
            dd(kn)
            for s in COPY_IN_ROUND.get(k, ()):
                a_copy(s)
            cc(k)
            p3(k, False)
            if 0 <= kd:
                p4(kd, 512, C)
                st0(kd, 0, C)
                p5(kd, 512, C, False)
                if kd >= 1:
                    st1(kd - 1, 0, C)
            if 2 <= k and k + 3 < 8:
                mm(k + 3)
            p1(ka, 0)
            p1(ka, 1)

        def y_part(k, lo, hi, cast_on_vector):
            p4(k, lo, hi)
            st0(k, lo, hi)
            p5(k, lo, hi, cast_on_vector)

        p4(4, 0, 512)
        st0(4, 0, 512)
        nm(7)
        p2(7)
        rec(6)
        p5(4, 0, 256, False)
        sq(7)
        p5(4, 256, 512, False)
        dd(7)
        p4(4, 512, 768)
        cc(6)
        p4(4, 768, C)
        st0(4, 512, C)
        p5(4, 512, C, False)
        st1(3, 0, C)
        p3(6, True)
        y_part(5, 0, 512, False)
        y_part(5, 512, C, False)
        st1(4, 0, C)
        rec(7)
        y_part(6, 0, 512, False)
        cc(7)
        y_part(6, 512, C, False)
        st1(5, 0, C)
        p3(7, True)
        y_part(7, 0, 512, False)
        st1(6, 0, C)
        y_part(7, 512, C, True)
        st1(7, 0, 512)
        st1(7, 512, C)
